import numpy as np
import ml_dtypes


def mxq(x, axis, fmt="e4m3"):
    dtype, down = {"e4m3": (ml_dtypes.float8_e4m3fn, 7), "e5m2": (ml_dtypes.float8_e5m2, 14)}[fmt]
    v = np.moveaxis(np.asarray(x, np.float32).astype(ml_dtypes.bfloat16).astype(np.float64), axis, -1)
    blocks = v.reshape(v.shape[:-1] + (-1, 32))
    amax = np.abs(blocks).max(-1, keepdims=True)
    byte = np.maximum(np.where(amax > 0, np.frexp(amax)[1] - 1 + 127, 0) - down, 1)
    scale = np.exp2(byte - 127.0)
    codes = (blocks / scale).astype(np.float32).astype(dtype).astype(np.float64)
    return np.moveaxis((codes * scale).reshape(v.shape), -1, axis)


WIDE = False


def mx_kscale(k):
    if not WIDE:
        return np.ones(k)
    levels = np.array([10, -10, 5, -5, 0])
    if k % 512:
        return np.exp2(np.random.permutation(np.resize(levels, k // 32))).repeat(32)
    a = np.empty((k // 512, 16))
    for p in range(k // 512):
        a[p, :8] = np.random.permutation(np.resize(levels, 8))
        for g in range(8):
            far = levels[np.abs(levels - a[p, g]) >= 10]
            a[p, g + 8] = far[np.random.randint(len(far))]
    return np.exp2(a.ravel()).repeat(32)


BF16 = ml_dtypes.bfloat16


def bf(x):
    return np.asarray(x, np.float32).astype(BF16)


def f64(x):
    return np.asarray(x).astype(np.float64)


E2M1 = np.array([0.0, 0.5, 1.0, 1.5, 2.0, 3.0, 4.0, 6.0, -0.0, -0.5, -1.0, -1.5, -2.0, -3.0, -4.0, -6.0])


def pack_weight(w, fmt):
    k, n = w.shape
    w = f64(bf(w)).reshape(k // 32, 32, n)
    amax = np.abs(w).max(1)
    if fmt == "e4m3":
        byte = np.frexp(amax)[1] - 1 + 127 - 7
    else:
        mant, ex = np.frexp(amax / 6.0)
        byte = np.where(mant > 0.5, ex, ex - 1) + 127
    byte = np.clip(np.where(amax > 0, byte, 1), 1, 254)
    scaled = (w * np.exp2(127.0 - byte)[:, None, :]).reshape(k, n).astype(np.float32)
    by_word = np.ascontiguousarray(scaled.reshape(k // 512, 128, 4, n).transpose(0, 1, 3, 2))
    if fmt == "e4m3":
        words = by_word.astype(ml_dtypes.float8_e4m3fn).view(np.uint8)
    else:
        c = by_word.astype(ml_dtypes.float4_e2m1fn).view(np.uint8) & 0xF
        words = c[..., 0::2] | (c[..., 1::2] << 4)
    return np.ascontiguousarray(words), np.ascontiguousarray(byte.astype(np.uint8).reshape(k // 512, 16, n))


def unpack_weight(words, scales, fmt):
    g, p, n, _ = words.shape
    if fmt == "e4m3":
        vals = np.ascontiguousarray(words).view(ml_dtypes.float8_e4m3fn).astype(np.float64)
    else:
        nib = np.empty((g, p, n, 4), np.uint8)
        nib[..., 0::2] = words & 0xF
        nib[..., 1::2] = words >> 4
        vals = E2M1[nib]
    vals = vals * np.repeat(np.exp2(scales.astype(np.float64) - 127.0), 8, axis=1)[..., None]
    return vals.transpose(0, 1, 3, 2).reshape(g * 512, n)


B, C, CI, N = 32, 512, 512, 256
A = np.sqrt(0.2 * N / np.sqrt(CI))
FMT = "e4m3"


def conv1x1(w, b, v):
    return (w @ mxq(v, 1, "e4m3")) + b[:, None]


def setup_inputs():
    s, u, t = mx_kscale(C), mx_kscale(C), mx_kscale(CI)
    r = np.random.standard_normal
    x = bf(r((B, C, N)) * s[None, :, None])
    x_2 = bf(r((B, C, N)) * u[None, :, None])
    theta_w = r((CI, C)) * A / np.sqrt(C) * t[:, None] / s[None, :]
    theta_b = bf(r(CI) * 0.2 * A * t)
    phi_w = r((CI, C)) * A / np.sqrt(C) / t[:, None] / u[None, :]
    phi_b = bf(r(CI) * 0.2 * A / t)
    theta_w_words, theta_w_scales = pack_weight(np.ascontiguousarray(theta_w.T), FMT)
    phi_w_words, phi_w_scales = pack_weight(np.ascontiguousarray(phi_w.T), FMT)
    return {"x": x,
            "x_2": x_2,
            "theta_w_words": theta_w_words,
            "theta_w_scales": theta_w_scales,
            "theta_b": theta_b,
            "phi_w_words": phi_w_words,
            "phi_w_scales": phi_w_scales,
            "phi_b": phi_b}


def reference(x, x_2, theta_w_words, theta_w_scales, theta_b, phi_w_words, phi_w_scales, phi_b):
    theta_w = unpack_weight(theta_w_words, theta_w_scales, FMT).T
    phi_w = unpack_weight(phi_w_words, phi_w_scales, FMT).T
    theta_x = conv1x1(theta_w, f64(theta_b), f64(x)).transpose(0, 2, 1)
    phi_x = conv1x1(phi_w, f64(phi_b), f64(x_2))
    return (mxq(theta_x, 2, "e4m3") @ mxq(phi_x, 1, "e4m3")) / N

@@ -1,0 +1,200 @@
+from contextlib import ExitStack
+
+import concourse.mybir as mybir
+
+BF16 = mybir.dt.bfloat16
+F32 = mybir.dt.float32
+I32 = mybir.dt.int32
+U32 = mybir.dt.uint32
+U8 = mybir.dt.uint8
+FP8X4 = mybir.dt.float8_e4m3fn_x4
+ACT = mybir.ActivationFunctionType
+
+P = 128
+PACK = 4
+BATCHES = 32
+CHANNELS = P * PACK
+POINTS = 256
+SIDES = 2
+ROUND_B = 2
+ROUNDS = BATCHES // ROUND_B
+COLS = ROUND_B * POINTS
+ROW_TILES = POINTS // P
+RUN = 4
+SCALAR_EVERY = 3
+LEAD = 2
+SCALAR_LEAD = LEAD + 2
+LOADS_AHEAD = SCALAR_LEAD + 1
+
+FLOPS = 2 * BATCHES * POINTS * CHANNELS * (2 * CHANNELS + POINTS)
+
+
+def regroup(nc, pool, rows, name, on_scalar=False):
+    grouped = pool.tile([P, 2, POINTS, PACK], BF16, align_bytes=64, name=name)
+    src = rows.rearrange("p g j (c i) -> p g c j i", i=RUN)
+    dst = grouped[:].rearrange("p g (c i) j -> p g c j i", i=RUN)
+    if on_scalar:
+        for g in range(2):
+            nc.scalar.copy(out=dst[:, g], in_=src[:, g])
+    else:
+        nc.vector.tensor_copy(out=dst, in_=src)
+    return grouped
+
+
+def quantise(nc, pool, grouped, name):
+    codes = pool.tile([P, 2, POINTS], U32, align_bytes=64, name="codes_" + name)
+    scales = pool.tile([P, 2, POINTS], U8, align_bytes=64, name="scales_" + name)
+    nc.vector.quantize_mx(
+        out=codes[:].rearrange("p g n -> p (g n)").bitcast(FP8X4),
+        scales=scales[:].rearrange("p g n -> p (g n)"),
+        in_=grouped[:].rearrange("p g n j -> p (g n j)"),
+    )
+    return codes, scales
+
+
+def tile_sgcam_pa_t_kernel(
+    tc, x, x_2, theta_w_words, theta_w_scales, theta_b, phi_w_words, phi_w_scales, phi_b, out
+):
+    nc = tc.nc
+    inputs = (x, x_2)
+    weight_words = (theta_w_words, phi_w_words)
+    weight_scales = (theta_w_scales, phi_w_scales)
+    biases = (theta_b, phi_b)
+    side_names = ("theta", "phi")
+
+    with ExitStack() as ctx:
+        consts = ctx.enter_context(tc.tile_pool(name="consts", bufs=1))
+        raw_pool = ctx.enter_context(tc.tile_pool(name="raw", bufs=LOADS_AHEAD + 1))
+        work = ctx.enter_context(tc.tile_pool(name="work", bufs=2))
+        planes_pool = ctx.enter_context(tc.tile_pool(name="planes", bufs=LEAD + 2))
+        result_pool = ctx.enter_context(tc.tile_pool(name="result", bufs=4))
+
+        raw = {}
+        grouped_in = {}
+        mx_in = {}
+        planes = {}
+
+        def load_round(r):
+            if r >= ROUNDS:
+                return
+            for side in range(SIDES):
+                raw[side, r] = raw_pool.tile([P, ROUND_B, PACK, POINTS], BF16, name="raw_" + side_names[side])
+                nc.sync.dma_start(
+                    out=raw[side, r][:].rearrange("p b j n -> p b (j n)"),
+                    in_=inputs[side][ROUND_B * r : ROUND_B * (r + 1)].rearrange("b (p j) n -> p b (j n)", j=PACK),
+                )
+
+        load_round(0)
+        w_codes_raw = consts.tile([P, SIDES, CHANNELS], I32, align_bytes=64, name="w_codes_raw")
+        w_planes_raw = consts.tile([P, SIDES, CHANNELS], U8, align_bytes=64, name="w_planes_raw")
+        w_codes = consts.tile([P, SIDES, CHANNELS], U32, align_bytes=64, name="w_codes")
+        w_planes = consts.tile([P, SIDES, CHANNELS], U8, align_bytes=64, name="w_planes")
+        nc.vector.memset(w_planes_raw[:].rearrange("p s c -> p (s c)").bitcast(I32), 0)
+        for side in range(SIDES):
+            nc.sync.dma_start(
+                out=w_codes_raw[:, side],
+                in_=weight_words[side][0].rearrange("p n t -> p (n t)").bitcast(I32),
+            )
+            for quadrant in range(4):
+                nc.sync.dma_start(
+                    out=w_planes_raw[32 * quadrant : 32 * quadrant + 4, side].bitcast(I32),
+                    in_=weight_scales[side][0, 4 * quadrant : 4 * quadrant + 4, :].bitcast(I32),
+                )
+        for r in range(1, LOADS_AHEAD):
+            load_round(r)
+
+        bias = []
+        for side in range(SIDES):
+            cols = consts.tile([P, PACK], BF16, name="bias_" + side_names[side])
+            nc.scalar.dma_start(out=cols[:], in_=biases[side].rearrange("(p t) -> p t", t=PACK))
+            bias.append(cols)
+
+        def permute_weights():
+            for side in range(SIDES):
+                nc.vector.tensor_copy(
+                    out=w_codes[:, side].bitcast(I32).rearrange("p (t m) -> p t m", t=PACK),
+                    in_=w_codes_raw[:, side].rearrange("p (m t) -> p t m", t=PACK),
+                )
+                nc.vector.tensor_copy(
+                    out=w_planes[:, side].rearrange("p (t m) -> p t m", t=PACK),
+                    in_=w_planes_raw[:, side].rearrange("p (m t) -> p t m", t=PACK),
+                )
+
+        feat_psum = ctx.enter_context(tc.psum_pool(name="feat_psum", bufs=6))
+        out_psum = ctx.enter_context(tc.psum_pool(name="out_psum", bufs=2))
+
+        def scalar_regroups(r):
+            if r < ROUNDS and r % SCALAR_EVERY == 0:
+                grouped_in[1, r] = regroup(nc, work, raw[1, r][:], "grouped_by_scalar", on_scalar=True)
+
+        def quantise_inputs(r):
+            for side in range(SIDES):
+                if (side, r) not in grouped_in:
+                    grouped_in[side, r] = regroup(nc, work, raw[side, r][:], "grouped_" + side_names[side])
+            for side in range(SIDES):
+                mx_in[side, r] = quantise(nc, work, grouped_in[side, r], side_names[side])
+
+        def project(r):
+            planes[r] = planes_pool.tile([P, PACK, SIDES, ROUND_B, POINTS], BF16, name="planes")
+            for side in range(SIDES):
+                codes, scales = mx_in[side, r]
+                for t in range(PACK):
+                    chans = slice(P * t, P * (t + 1))
+                    acc = feat_psum.tile([P, COLS], F32, name="acc")
+                    nc.tensor.matmul_mx(
+                        out=acc[:],
+                        lhsT=w_codes[:, side, chans].bitcast(FP8X4),
+                        lhsT_scale=w_planes[:, side, chans],
+                        rhs=codes[:].rearrange("p b n -> p (b n)").bitcast(FP8X4),
+                        rhs_scale=scales[:].rearrange("p b n -> p (b n)"),
+                        start=True,
+                        stop=True,
+                    )
+                    nc.scalar.activation(
+                        out=planes[r][:, t, side].rearrange("p b n -> p (b n)"),
+                        in_=acc[:],
+                        func=ACT.Identity,
+                        bias=bias[side][:, t : t + 1],
+                        scale=1.0,
+                    )
+
+        def affinity(r):
+            grouped = []
+            for i in range(ROUND_B):
+                rows = planes[r][:, :, :, i, :].rearrange("p t s n -> p s t n")
+                grouped.append(regroup(nc, work, rows, "grouped_batch%d" % i))
+            for i in range(ROUND_B):
+                codes, scales = quantise(nc, work, grouped[i], "batch%d" % i)
+                prod = out_psum.tile([P, ROW_TILES, POINTS], F32, name="prod")
+                for c in range(ROW_TILES):
+                    rows_c = slice(P * c, P * (c + 1))
+                    nc.tensor.matmul_mx(
+                        out=prod[:, c, :],
+                        lhsT=codes[:, 0, rows_c].bitcast(FP8X4),
+                        lhsT_scale=scales[:, 0, rows_c],
+                        rhs=codes[:, 1, :].bitcast(FP8X4),
+                        rhs_scale=scales[:, 1, :],
+                        start=True,
+                        stop=True,
+                    )
+                result = result_pool.tile([P, ROW_TILES, POINTS], F32, name="result")
+                nc.scalar.activation(out=result[:], in_=prod[:], func=ACT.Copy, scale=1.0 / POINTS)
+                nc.sync.dma_start(out=out[ROUND_B * r + i].rearrange("(c p) m -> p c m", p=P), in_=result[:])
+
+        with tc.manual_schedule():
+            scalar_regroups(0)
+            for r in range(LEAD):
+                quantise_inputs(r)
+                if r == 0:
+                    permute_weights()
+                project(r)
+                scalar_regroups(r + 1)
+            for r in range(LEAD + 1, SCALAR_LEAD):
+                scalar_regroups(r)
+            for r in range(ROUNDS):
+                load_round(r + LOADS_AHEAD)
+                if r + LEAD < ROUNDS:
+                    quantise_inputs(r + LEAD)
+                    project(r + LEAD)
+                affinity(r)
+                scalar_regroups(r + SCALAR_LEAD)

@@ -1,6 +1,7 @@
 from contextlib import ExitStack
 
 import concourse.mybir as mybir
+from concourse.masks import make_identity
 
 BF16 = mybir.dt.bfloat16
 F32 = mybir.dt.float32
@@ -21,23 +22,18 @@ ROUNDS = BATCHES // ROUND_B
 COLS = ROUND_B * POINTS
 ROW_TILES = POINTS // P
 RUN = 4
-SCALAR_EVERY = 3
 LEAD = 2
-SCALAR_LEAD = LEAD + 2
-LOADS_AHEAD = SCALAR_LEAD + 1
+SPREAD_LEAD = LEAD + 1
+LOADS_AHEAD = SPREAD_LEAD + 2
 
 FLOPS = 2 * BATCHES * POINTS * CHANNELS * (2 * CHANNELS + POINTS)
 
 
-def regroup(nc, pool, rows, name, on_scalar=False):
+def regroup(nc, pool, rows, name):
     grouped = pool.tile([P, 2, POINTS, PACK], BF16, align_bytes=64, name=name)
     src = rows.rearrange("p g j (c i) -> p g c j i", i=RUN)
     dst = grouped[:].rearrange("p g (c i) j -> p g c j i", i=RUN)
-    if on_scalar:
-        for g in range(2):
-            nc.scalar.copy(out=dst[:, g], in_=src[:, g])
-    else:
-        nc.vector.tensor_copy(out=dst, in_=src)
+    nc.vector.tensor_copy(out=dst, in_=src)
     return grouped
 
 
@@ -68,6 +64,7 @@ def tile_sgcam_pa_t_kernel(
         work = ctx.enter_context(tc.tile_pool(name="work", bufs=2))
         planes_pool = ctx.enter_context(tc.tile_pool(name="planes", bufs=LEAD + 2))
         result_pool = ctx.enter_context(tc.tile_pool(name="result", bufs=4))
+        psum = ctx.enter_context(tc.psum_pool(name="psum", bufs=8))
 
         raw = {}
         grouped_in = {}
@@ -103,34 +100,46 @@ def tile_sgcam_pa_t_kernel(
         for r in range(1, LOADS_AHEAD):
             load_round(r)
 
+        identity = consts.tile([P, P], BF16, name="identity")
+        make_identity(nc, identity[:])
         bias = []
         for side in range(SIDES):
             cols = consts.tile([P, PACK], BF16, name="bias_" + side_names[side])
             nc.scalar.dma_start(out=cols[:], in_=biases[side].rearrange("(p t) -> p t", t=PACK))
             bias.append(cols)
 
-        def permute_weights():
-            for side in range(SIDES):
-                nc.vector.tensor_copy(
-                    out=w_codes[:, side].bitcast(I32).rearrange("p (t m) -> p t m", t=PACK),
-                    in_=w_codes_raw[:, side].rearrange("p (m t) -> p t m", t=PACK),
-                )
-                nc.vector.tensor_copy(
-                    out=w_planes[:, side].rearrange("p (t m) -> p t m", t=PACK),
-                    in_=w_planes_raw[:, side].rearrange("p (m t) -> p t m", t=PACK),
-                )
+        def permute_weights(side):
+            nc.vector.tensor_copy(
+                out=w_codes[:, side].bitcast(I32).rearrange("p (t m) -> p t m", t=PACK),
+                in_=w_codes_raw[:, side].rearrange("p (m t) -> p t m", t=PACK),
+            )
+            nc.vector.tensor_copy(
+                out=w_planes[:, side].rearrange("p (t m) -> p t m", t=PACK),
+                in_=w_planes_raw[:, side].rearrange("p (m t) -> p t m", t=PACK),
+            )
 
-        feat_psum = ctx.enter_context(tc.psum_pool(name="feat_psum", bufs=6))
-        out_psum = ctx.enter_context(tc.psum_pool(name="out_psum", bufs=2))
+        def spread(r):
+            if r >= ROUNDS:
+                return
+            grouped = work.tile([P, ROUND_B, POINTS, PACK], BF16, align_bytes=64, name="grouped_phi")
+            for b in range(ROUND_B):
+                bank = psum.tile([P, POINTS, PACK], BF16, name="bank")
+                for c in range(ROW_TILES):
+                    points = slice(P * c, P * (c + 1))
+                    nc.tensor.matmul(
+                        bank[:, points, :],
+                        lhsT=identity[:],
+                        rhs=raw[1, r][:, b, :, points].rearrange("p j n -> p n j"),
+                        start=True,
+                        stop=True,
+                    )
+                nc.scalar.copy(out=grouped[:, b], in_=bank[:])
+            grouped_in[1, r] = grouped
 
-        def scalar_regroups(r):
-            if r < ROUNDS and r % SCALAR_EVERY == 0:
-                grouped_in[1, r] = regroup(nc, work, raw[1, r][:], "grouped_by_scalar", on_scalar=True)
+        def regroup_x(r):
+            grouped_in[0, r] = regroup(nc, work, raw[0, r][:], "grouped_theta")
 
         def quantise_inputs(r):
-            for side in range(SIDES):
-                if (side, r) not in grouped_in:
-                    grouped_in[side, r] = regroup(nc, work, raw[side, r][:], "grouped_" + side_names[side])
             for side in range(SIDES):
                 mx_in[side, r] = quantise(nc, work, grouped_in[side, r], side_names[side])
 
@@ -140,7 +149,7 @@ def tile_sgcam_pa_t_kernel(
                 codes, scales = mx_in[side, r]
                 for t in range(PACK):
                     chans = slice(P * t, P * (t + 1))
-                    acc = feat_psum.tile([P, COLS], F32, name="acc")
+                    acc = psum.tile([P, COLS], F32, name="bank")
                     nc.tensor.matmul_mx(
                         out=acc[:],
                         lhsT=w_codes[:, side, chans].bitcast(FP8X4),
@@ -158,14 +167,16 @@ def tile_sgcam_pa_t_kernel(
                         scale=1.0,
                     )
 
-        def affinity(r):
-            grouped = []
-            for i in range(ROUND_B):
-                rows = planes[r][:, :, :, i, :].rearrange("p t s n -> p s t n")
-                grouped.append(regroup(nc, work, rows, "grouped_batch%d" % i))
+        def regroup_features(r):
+            return [
+                regroup(nc, work, planes[r][:, :, :, i, :].rearrange("p t s n -> p s t n"), "grouped_batch%d" % i)
+                for i in range(ROUND_B)
+            ]
+
+        def affinity(r, grouped):
             for i in range(ROUND_B):
                 codes, scales = quantise(nc, work, grouped[i], "batch%d" % i)
-                prod = out_psum.tile([P, ROW_TILES, POINTS], F32, name="prod")
+                prod = psum.tile([P, ROW_TILES, POINTS], F32, name="bank")
                 for c in range(ROW_TILES):
                     rows_c = slice(P * c, P * (c + 1))
                     nc.tensor.matmul_mx(
@@ -182,19 +193,22 @@ def tile_sgcam_pa_t_kernel(
                 nc.sync.dma_start(out=out[ROUND_B * r + i].rearrange("(c p) m -> p c m", p=P), in_=result[:])
 
         with tc.manual_schedule():
-            scalar_regroups(0)
+            spread(0)
+            regroup_x(0)
+            permute_weights(0)
+            permute_weights(1)
             for r in range(LEAD):
+                spread(r + 1)
                 quantise_inputs(r)
-                if r == 0:
-                    permute_weights()
+                regroup_x(r + 1)
                 project(r)
-                scalar_regroups(r + 1)
-            for r in range(LEAD + 1, SCALAR_LEAD):
-                scalar_regroups(r)
             for r in range(ROUNDS):
                 load_round(r + LOADS_AHEAD)
+                spread(r + SPREAD_LEAD)
+                grouped = regroup_features(r)
                 if r + LEAD < ROUNDS:
                     quantise_inputs(r + LEAD)
+                    if r + LEAD + 1 < ROUNDS:
+                        regroup_x(r + LEAD + 1)
                     project(r + LEAD)
-                affinity(r)
-                scalar_regroups(r + SCALAR_LEAD)
+                affinity(r, grouped)

@@ -127,9 +127,9 @@ def tile_sgcam_pa_t_kernel(
                 for c in range(ROW_TILES):
                     points = slice(P * c, P * (c + 1))
                     nc.tensor.matmul(
-                        bank[:, points, :],
+                        bank[:, points, :].rearrange("p n j -> p j n"),
                         lhsT=identity[:],
-                        rhs=raw[1, r][:, b, :, points].rearrange("p j n -> p n j"),
+                        rhs=raw[1, r][:, b, :, points],
                         start=True,
                         stop=True,
                     )

@@ -10,6 +10,7 @@ U32 = mybir.dt.uint32
 U8 = mybir.dt.uint8
 FP8X4 = mybir.dt.float8_e4m3fn_x4
 ACT = mybir.ActivationFunctionType
+ALU = mybir.AluOpType
 
 P = 128
 PACK = 4
@@ -21,10 +22,11 @@ ROUND_B = 2
 ROUNDS = BATCHES // ROUND_B
 COLS = ROUND_B * POINTS
 ROW_TILES = POINTS // P
-RUN = 4
-LEAD = 2
-SPREAD_LEAD = LEAD + 1
-LOADS_AHEAD = SPREAD_LEAD + 2
+RUN = 8
+GROUP_LEAD = 2
+LOADS_AHEAD = GROUP_LEAD + 2
+VECTOR_X2_ROUND = 1
+VECTOR_OUT_ROUNDS = 14
 
 FLOPS = 2 * BATCHES * POINTS * CHANNELS * (2 * CHANNELS + POINTS)
 
@@ -62,14 +64,14 @@ def tile_sgcam_pa_t_kernel(
         consts = ctx.enter_context(tc.tile_pool(name="consts", bufs=1))
         raw_pool = ctx.enter_context(tc.tile_pool(name="raw", bufs=LOADS_AHEAD + 1))
         work = ctx.enter_context(tc.tile_pool(name="work", bufs=2))
-        planes_pool = ctx.enter_context(tc.tile_pool(name="planes", bufs=LEAD + 2))
+        planes_pool = ctx.enter_context(tc.tile_pool(name="planes", bufs=3))
         result_pool = ctx.enter_context(tc.tile_pool(name="result", bufs=4))
         psum = ctx.enter_context(tc.psum_pool(name="psum", bufs=8))
 
         raw = {}
         grouped_in = {}
-        mx_in = {}
         planes = {}
+        waiting = []
 
         def load_round(r):
             if r >= ROUNDS:
@@ -121,6 +123,9 @@ def tile_sgcam_pa_t_kernel(
         def spread(r):
             if r >= ROUNDS:
                 return
+            if r == VECTOR_X2_ROUND:
+                grouped_in[1, r] = regroup(nc, work, raw[1, r][:], "grouped_phi")
+                return
             grouped = work.tile([P, ROUND_B, POINTS, PACK], BF16, align_bytes=64, name="grouped_phi")
             for b in range(ROUND_B):
                 bank = psum.tile([P, POINTS, PACK], BF16, name="bank")
@@ -137,35 +142,32 @@ def tile_sgcam_pa_t_kernel(
             grouped_in[1, r] = grouped
 
         def regroup_x(r):
-            grouped_in[0, r] = regroup(nc, work, raw[0, r][:], "grouped_theta")
+            if r < ROUNDS:
+                grouped_in[0, r] = regroup(nc, work, raw[0, r][:], "grouped_theta")
 
-        def quantise_inputs(r):
-            for side in range(SIDES):
-                mx_in[side, r] = quantise(nc, work, grouped_in[side, r], side_names[side])
-
-        def project(r):
-            planes[r] = planes_pool.tile([P, PACK, SIDES, ROUND_B, POINTS], BF16, name="planes")
-            for side in range(SIDES):
-                codes, scales = mx_in[side, r]
-                for t in range(PACK):
-                    chans = slice(P * t, P * (t + 1))
-                    acc = psum.tile([P, COLS], F32, name="bank")
-                    nc.tensor.matmul_mx(
-                        out=acc[:],
-                        lhsT=w_codes[:, side, chans].bitcast(FP8X4),
-                        lhsT_scale=w_planes[:, side, chans],
-                        rhs=codes[:].rearrange("p b n -> p (b n)").bitcast(FP8X4),
-                        rhs_scale=scales[:].rearrange("p b n -> p (b n)"),
-                        start=True,
-                        stop=True,
-                    )
-                    nc.scalar.activation(
-                        out=planes[r][:, t, side].rearrange("p b n -> p (b n)"),
-                        in_=acc[:],
-                        func=ACT.Identity,
-                        bias=bias[side][:, t : t + 1],
-                        scale=1.0,
-                    )
+        def project(r, side):
+            if side == 0:
+                planes[r] = planes_pool.tile([P, PACK, SIDES, ROUND_B, POINTS], BF16, name="planes")
+            codes, scales = quantise(nc, work, grouped_in[side, r], side_names[side])
+            for t in range(PACK):
+                chans = slice(P * t, P * (t + 1))
+                acc = psum.tile([P, COLS], F32, name="bank")
+                nc.tensor.matmul_mx(
+                    out=acc[:],
+                    lhsT=w_codes[:, side, chans].bitcast(FP8X4),
+                    lhsT_scale=w_planes[:, side, chans],
+                    rhs=codes[:].rearrange("p b n -> p (b n)").bitcast(FP8X4),
+                    rhs_scale=scales[:].rearrange("p b n -> p (b n)"),
+                    start=True,
+                    stop=True,
+                )
+                nc.scalar.activation(
+                    out=planes[r][:, t, side].rearrange("p b n -> p (b n)"),
+                    in_=acc[:],
+                    func=ACT.Identity,
+                    bias=bias[side][:, t : t + 1],
+                    scale=1.0,
+                )
 
         def regroup_features(r):
             return [
@@ -188,27 +190,42 @@ def tile_sgcam_pa_t_kernel(
                         start=True,
                         stop=True,
                     )
-                result = result_pool.tile([P, ROW_TILES, POINTS], F32, name="result")
+                if i == ROUND_B - 1 and r < VECTOR_OUT_ROUNDS:
+                    waiting.append((r, i, prod))
+                else:
+                    deliver(r, i, prod, on_vector=False)
+
+        def deliver(r, i, prod, on_vector):
+            result = result_pool.tile([P, ROW_TILES, POINTS], F32, name="result")
+            if on_vector:
+                nc.vector.tensor_scalar(
+                    out=result[:], in0=prod[:], scalar1=1.0 / POINTS, scalar2=None, op0=ALU.mult
+                )
+            else:
                 nc.scalar.activation(out=result[:], in_=prod[:], func=ACT.Copy, scale=1.0 / POINTS)
-                nc.sync.dma_start(out=out[ROUND_B * r + i].rearrange("(c p) m -> p c m", p=P), in_=result[:])
+            nc.sync.dma_start(out=out[ROUND_B * r + i].rearrange("(c p) m -> p c m", p=P), in_=result[:])
+
+        def deliver_waiting():
+            for r, i, prod in waiting:
+                deliver(r, i, prod, on_vector=True)
+            waiting.clear()
 
         with tc.manual_schedule():
             spread(0)
             regroup_x(0)
             permute_weights(0)
+            project(0, 0)
             permute_weights(1)
-            for r in range(LEAD):
-                spread(r + 1)
-                quantise_inputs(r)
-                regroup_x(r + 1)
-                project(r)
+            project(0, 1)
+            regroup_x(1)
+            spread(1)
             for r in range(ROUNDS):
                 load_round(r + LOADS_AHEAD)
-                spread(r + SPREAD_LEAD)
+                if r + 1 < ROUNDS:
+                    project(r + 1, 0)
+                    project(r + 1, 1)
+                spread(r + GROUP_LEAD)
                 grouped = regroup_features(r)
-                if r + LEAD < ROUNDS:
-                    quantise_inputs(r + LEAD)
-                    if r + LEAD + 1 < ROUNDS:
-                        regroup_x(r + LEAD + 1)
-                    project(r + LEAD)
+                deliver_waiting()
+                regroup_x(r + GROUP_LEAD)
                 affinity(r, grouped)

@@ -24,9 +24,10 @@ COLS = ROUND_B * POINTS
 ROW_TILES = POINTS // P
 RUN = 8
 GROUP_LEAD = 2
-LOADS_AHEAD = GROUP_LEAD + 2
+SPREAD_LEAD = GROUP_LEAD + 1
+LOADS_AHEAD = SPREAD_LEAD + 2
 VECTOR_X2_ROUND = 1
-VECTOR_OUT_ROUNDS = 14
+DIRECT_ROUNDS = range(2, 14)
 
 FLOPS = 2 * BATCHES * POINTS * CHANNELS * (2 * CHANNELS + POINTS)
 
@@ -37,6 +38,12 @@ def regroup(nc, pool, rows, name):
     dst = grouped[:].rearrange("p g (c i) j -> p g c j i", i=RUN)
     nc.vector.tensor_copy(out=dst, in_=src)
     return grouped
+
+
+def regroup_one(nc, grouped, rows):
+    nc.vector.tensor_copy(
+        out=grouped.rearrange("p (c i) j -> p c j i", i=RUN), in_=rows.rearrange("p j (c i) -> p c j i", i=RUN)
+    )
 
 
 def quantise(nc, pool, grouped, name):
@@ -64,6 +71,8 @@ def tile_sgcam_pa_t_kernel(
         consts = ctx.enter_context(tc.tile_pool(name="consts", bufs=1))
         raw_pool = ctx.enter_context(tc.tile_pool(name="raw", bufs=LOADS_AHEAD + 1))
         work = ctx.enter_context(tc.tile_pool(name="work", bufs=2))
+        spread_pool = ctx.enter_context(tc.tile_pool(name="spread", bufs=SPREAD_LEAD))
+        feat_pool = ctx.enter_context(tc.tile_pool(name="feat", bufs=3))
         planes_pool = ctx.enter_context(tc.tile_pool(name="planes", bufs=3))
         result_pool = ctx.enter_context(tc.tile_pool(name="result", bufs=4))
         psum = ctx.enter_context(tc.psum_pool(name="psum", bufs=8))
@@ -71,7 +80,8 @@ def tile_sgcam_pa_t_kernel(
         raw = {}
         grouped_in = {}
         planes = {}
-        waiting = []
+        grouped_feat = {}
+        direct_banks = {}
 
         def load_round(r):
             if r >= ROUNDS:
@@ -124,9 +134,9 @@ def tile_sgcam_pa_t_kernel(
             if r >= ROUNDS:
                 return
             if r == VECTOR_X2_ROUND:
-                grouped_in[1, r] = regroup(nc, work, raw[1, r][:], "grouped_phi")
+                grouped_in[1, r] = regroup(nc, spread_pool, raw[1, r][:], "grouped_phi")
                 return
-            grouped = work.tile([P, ROUND_B, POINTS, PACK], BF16, align_bytes=64, name="grouped_phi")
+            grouped = spread_pool.tile([P, ROUND_B, POINTS, PACK], BF16, align_bytes=64, name="grouped_phi")
             for b in range(ROUND_B):
                 bank = psum.tile([P, POINTS, PACK], BF16, name="bank")
                 for c in range(ROW_TILES):
@@ -145,39 +155,77 @@ def tile_sgcam_pa_t_kernel(
             if r < ROUNDS:
                 grouped_in[0, r] = regroup(nc, work, raw[0, r][:], "grouped_theta")
 
+        def multiply(acc, side, t, codes, scales):
+            chans = slice(P * t, P * (t + 1))
+            nc.tensor.matmul_mx(
+                out=acc,
+                lhsT=w_codes[:, side, chans].bitcast(FP8X4),
+                lhsT_scale=w_planes[:, side, chans],
+                rhs=codes.bitcast(FP8X4),
+                rhs_scale=scales,
+                start=True,
+                stop=True,
+            )
+
+        def add_bias(plane, acc, side, t):
+            nc.scalar.activation(
+                out=plane, in_=acc, func=ACT.Identity, bias=bias[side][:, t : t + 1], scale=1.0
+            )
+
         def project(r, side):
             if side == 0:
                 planes[r] = planes_pool.tile([P, PACK, SIDES, ROUND_B, POINTS], BF16, name="planes")
             codes, scales = quantise(nc, work, grouped_in[side, r], side_names[side])
-            for t in range(PACK):
-                chans = slice(P * t, P * (t + 1))
-                acc = psum.tile([P, COLS], F32, name="bank")
-                nc.tensor.matmul_mx(
-                    out=acc[:],
-                    lhsT=w_codes[:, side, chans].bitcast(FP8X4),
-                    lhsT_scale=w_planes[:, side, chans],
-                    rhs=codes[:].rearrange("p b n -> p (b n)").bitcast(FP8X4),
-                    rhs_scale=scales[:].rearrange("p b n -> p (b n)"),
-                    start=True,
-                    stop=True,
+            if side == 1 and r in DIRECT_ROUNDS:
+                for pair in range(PACK // 2):
+                    acc = psum.tile([P, 2, POINTS], F32, name="bank")
+                    for k in range(2):
+                        multiply(acc[:, k, :], side, 2 * pair + k, codes[:, 0, :], scales[:, 0, :])
+                    for k in range(2):
+                        add_bias(planes[r][:, 2 * pair + k, side, 0, :], acc[:, k, :], side, 2 * pair + k)
+                direct_banks[r] = []
+                for c in range(ROW_TILES):
+                    points = slice(P * c, P * (c + 1))
+                    acc = psum.tile([P, PACK, P], F32, name="bank")
+                    for t in range(PACK):
+                        multiply(acc[:, t, :], side, t, codes[:, 1, points], scales[:, 1, points])
+                    direct_banks[r].append(acc)
+            else:
+                for t in range(PACK):
+                    acc = psum.tile([P, COLS], F32, name="bank")
+                    multiply(
+                        acc[:],
+                        side,
+                        t,
+                        codes[:].rearrange("p b n -> p (b n)"),
+                        scales[:].rearrange("p b n -> p (b n)"),
+                    )
+                    add_bias(planes[r][:, t, side].rearrange("p b n -> p (b n)"), acc[:], side, t)
+
+        def empty_direct(r):
+            if r not in direct_banks:
+                return
+            grouped = feat_pool.tile([P, SIDES, POINTS, PACK], BF16, align_bytes=64, name="grouped_batch1")
+            for c in range(ROW_TILES):
+                nc.vector.tensor_tensor(
+                    out=grouped[:, 1, P * c : P * (c + 1), :],
+                    in0=direct_banks[r][c][:].rearrange("p t n -> p n t"),
+                    in1=bias[1][:].unsqueeze(1).to_broadcast([P, P, PACK]),
+                    op=ALU.add,
                 )
-                nc.scalar.activation(
-                    out=planes[r][:, t, side].rearrange("p b n -> p (b n)"),
-                    in_=acc[:],
-                    func=ACT.Identity,
-                    bias=bias[side][:, t : t + 1],
-                    scale=1.0,
-                )
+            grouped_feat[1, r] = grouped
 
         def regroup_features(r):
-            return [
-                regroup(nc, work, planes[r][:, :, :, i, :].rearrange("p t s n -> p s t n"), "grouped_batch%d" % i)
-                for i in range(ROUND_B)
-            ]
-
-        def affinity(r, grouped):
             for i in range(ROUND_B):
-                codes, scales = quantise(nc, work, grouped[i], "batch%d" % i)
+                if (i, r) in grouped_feat:
+                    regroup_one(nc, grouped_feat[i, r][:, 0], planes[r][:, :, 0, i, :])
+                else:
+                    rows = planes[r][:, :, :, i, :].rearrange("p t s n -> p s t n")
+                    grouped_feat[i, r] = regroup(nc, feat_pool, rows, "grouped_batch%d" % i)
+
+        def affinity(r):
+            for i in range(ROUND_B):
+                codes, scales = quantise(nc, work, grouped_feat[i, r], "batch%d" % i)
                 prod = psum.tile([P, ROW_TILES, POINTS], F32, name="bank")
                 for c in range(ROW_TILES):
                     rows_c = slice(P * c, P * (c + 1))
@@ -190,25 +238,9 @@ def tile_sgcam_pa_t_kernel(
                         start=True,
                         stop=True,
                     )
-                if i == ROUND_B - 1 and r < VECTOR_OUT_ROUNDS:
-                    waiting.append((r, i, prod))
-                else:
-                    deliver(r, i, prod, on_vector=False)
-
-        def deliver(r, i, prod, on_vector):
-            result = result_pool.tile([P, ROW_TILES, POINTS], F32, name="result")
-            if on_vector:
-                nc.vector.tensor_scalar(
-                    out=result[:], in0=prod[:], scalar1=1.0 / POINTS, scalar2=None, op0=ALU.mult
-                )
-            else:
+                result = result_pool.tile([P, ROW_TILES, POINTS], F32, name="result")
                 nc.scalar.activation(out=result[:], in_=prod[:], func=ACT.Copy, scale=1.0 / POINTS)
-            nc.sync.dma_start(out=out[ROUND_B * r + i].rearrange("(c p) m -> p c m", p=P), in_=result[:])
-
-        def deliver_waiting():
-            for r, i, prod in waiting:
-                deliver(r, i, prod, on_vector=True)
-            waiting.clear()
+                nc.sync.dma_start(out=out[ROUND_B * r + i].rearrange("(c p) m -> p c m", p=P), in_=result[:])
 
         with tc.manual_schedule():
             spread(0)
@@ -218,14 +250,15 @@ def tile_sgcam_pa_t_kernel(
             permute_weights(1)
             project(0, 1)
             regroup_x(1)
-            spread(1)
+            for r in range(1, SPREAD_LEAD):
+                spread(r)
             for r in range(ROUNDS):
                 load_round(r + LOADS_AHEAD)
                 if r + 1 < ROUNDS:
                     project(r + 1, 0)
                     project(r + 1, 1)
-                spread(r + GROUP_LEAD)
-                grouped = regroup_features(r)
-                deliver_waiting()
+                spread(r + SPREAD_LEAD)
+                regroup_features(r)
                 regroup_x(r + GROUP_LEAD)
-                affinity(r, grouped)
+                empty_direct(r + 1)
+                affinity(r)

@@ -23,11 +23,10 @@ ROUNDS = BATCHES // ROUND_B
 COLS = ROUND_B * POINTS
 ROW_TILES = POINTS // P
 RUN = 8
-GROUP_LEAD = 2
-SPREAD_LEAD = GROUP_LEAD + 1
-LOADS_AHEAD = SPREAD_LEAD + 2
-VECTOR_X2_ROUND = 1
-DIRECT_ROUNDS = range(2, 14)
+LEAD = 2
+GROUP_LEAD = LEAD + 1
+LOADS_AHEAD = GROUP_LEAD + 2
+DIRECT_EVERY = 3
 
 FLOPS = 2 * BATCHES * POINTS * CHANNELS * (2 * CHANNELS + POINTS)
 
@@ -70,10 +69,10 @@ def tile_sgcam_pa_t_kernel(
     with ExitStack() as ctx:
         consts = ctx.enter_context(tc.tile_pool(name="consts", bufs=1))
         raw_pool = ctx.enter_context(tc.tile_pool(name="raw", bufs=LOADS_AHEAD + 1))
-        work = ctx.enter_context(tc.tile_pool(name="work", bufs=2))
-        spread_pool = ctx.enter_context(tc.tile_pool(name="spread", bufs=SPREAD_LEAD))
+        work = ctx.enter_context(tc.tile_pool(name="work", bufs=3))
+        in_pool = ctx.enter_context(tc.tile_pool(name="in", bufs=3))
         feat_pool = ctx.enter_context(tc.tile_pool(name="feat", bufs=3))
-        planes_pool = ctx.enter_context(tc.tile_pool(name="planes", bufs=3))
+        planes_pool = ctx.enter_context(tc.tile_pool(name="planes", bufs=LEAD + 2))
         result_pool = ctx.enter_context(tc.tile_pool(name="result", bufs=4))
         psum = ctx.enter_context(tc.psum_pool(name="psum", bufs=8))
 
@@ -83,34 +82,33 @@ def tile_sgcam_pa_t_kernel(
         grouped_feat = {}
         direct_banks = {}
 
-        def load_round(r):
-            if r >= ROUNDS:
-                return
-            for side in range(SIDES):
+        def load(side, r):
+            if r < ROUNDS:
                 raw[side, r] = raw_pool.tile([P, ROUND_B, PACK, POINTS], BF16, name="raw_" + side_names[side])
                 nc.sync.dma_start(
                     out=raw[side, r][:].rearrange("p b j n -> p b (j n)"),
                     in_=inputs[side][ROUND_B * r : ROUND_B * (r + 1)].rearrange("b (p j) n -> p b (j n)", j=PACK),
                 )
 
-        load_round(0)
         w_codes_raw = consts.tile([P, SIDES, CHANNELS], I32, align_bytes=64, name="w_codes_raw")
         w_planes_raw = consts.tile([P, SIDES, CHANNELS], U8, align_bytes=64, name="w_planes_raw")
         w_codes = consts.tile([P, SIDES, CHANNELS], U32, align_bytes=64, name="w_codes")
         w_planes = consts.tile([P, SIDES, CHANNELS], U8, align_bytes=64, name="w_planes")
         nc.vector.memset(w_planes_raw[:].rearrange("p s c -> p (s c)").bitcast(I32), 0)
         for side in range(SIDES):
-            nc.sync.dma_start(
-                out=w_codes_raw[:, side],
-                in_=weight_words[side][0].rearrange("p n t -> p (n t)").bitcast(I32),
-            )
             for quadrant in range(4):
                 nc.sync.dma_start(
                     out=w_planes_raw[32 * quadrant : 32 * quadrant + 4, side].bitcast(I32),
                     in_=weight_scales[side][0, 4 * quadrant : 4 * quadrant + 4, :].bitcast(I32),
                 )
+            nc.sync.dma_start(
+                out=w_codes_raw[:, side],
+                in_=weight_words[side][0].rearrange("p n t -> p (n t)").bitcast(I32),
+            )
+            load(side, 0)
         for r in range(1, LOADS_AHEAD):
-            load_round(r)
+            for side in range(SIDES):
+                load(side, r)
 
         identity = consts.tile([P, P], BF16, name="identity")
         make_identity(nc, identity[:])
@@ -133,10 +131,10 @@ def tile_sgcam_pa_t_kernel(
         def spread(r):
             if r >= ROUNDS:
                 return
-            if r == VECTOR_X2_ROUND:
-                grouped_in[1, r] = regroup(nc, spread_pool, raw[1, r][:], "grouped_phi")
+            if r < LEAD:
+                grouped_in[1, r] = regroup(nc, in_pool, raw[1, r][:], "grouped_phi")
                 return
-            grouped = spread_pool.tile([P, ROUND_B, POINTS, PACK], BF16, align_bytes=64, name="grouped_phi")
+            grouped = in_pool.tile([P, ROUND_B, POINTS, PACK], BF16, align_bytes=64, name="grouped_phi")
             for b in range(ROUND_B):
                 bank = psum.tile([P, POINTS, PACK], BF16, name="bank")
                 for c in range(ROW_TILES):
@@ -153,7 +151,7 @@ def tile_sgcam_pa_t_kernel(
 
         def regroup_x(r):
             if r < ROUNDS:
-                grouped_in[0, r] = regroup(nc, work, raw[0, r][:], "grouped_theta")
+                grouped_in[0, r] = regroup(nc, in_pool, raw[0, r][:], "grouped_theta")
 
         def multiply(acc, side, t, codes, scales):
             chans = slice(P * t, P * (t + 1))
@@ -172,11 +170,14 @@ def tile_sgcam_pa_t_kernel(
                 out=plane, in_=acc, func=ACT.Identity, bias=bias[side][:, t : t + 1], scale=1.0
             )
 
+        def is_direct(r):
+            return r < ROUNDS and r % DIRECT_EVERY != 0
+
         def project(r, side):
             if side == 0:
                 planes[r] = planes_pool.tile([P, PACK, SIDES, ROUND_B, POINTS], BF16, name="planes")
             codes, scales = quantise(nc, work, grouped_in[side, r], side_names[side])
-            if side == 1 and r in DIRECT_ROUNDS:
+            if side == 1 and is_direct(r):
                 for pair in range(PACK // 2):
                     acc = psum.tile([P, 2, POINTS], F32, name="bank")
                     for k in range(2):
@@ -203,7 +204,7 @@ def tile_sgcam_pa_t_kernel(
                     add_bias(planes[r][:, t, side].rearrange("p b n -> p (b n)"), acc[:], side, t)
 
         def empty_direct(r):
-            if r not in direct_banks:
+            if not is_direct(r):
                 return
             grouped = feat_pool.tile([P, SIDES, POINTS, PACK], BF16, align_bytes=64, name="grouped_batch1")
             for c in range(ROW_TILES):
@@ -215,13 +216,12 @@ def tile_sgcam_pa_t_kernel(
                 )
             grouped_feat[1, r] = grouped
 
-        def regroup_features(r):
-            for i in range(ROUND_B):
-                if (i, r) in grouped_feat:
-                    regroup_one(nc, grouped_feat[i, r][:, 0], planes[r][:, :, 0, i, :])
-                else:
-                    rows = planes[r][:, :, :, i, :].rearrange("p t s n -> p s t n")
-                    grouped_feat[i, r] = regroup(nc, feat_pool, rows, "grouped_batch%d" % i)
+        def regroup_features(r, i):
+            if (i, r) in grouped_feat:
+                regroup_one(nc, grouped_feat[i, r][:, 0], planes[r][:, :, 0, i, :])
+            else:
+                rows = planes[r][:, :, :, i, :].rearrange("p t s n -> p s t n")
+                grouped_feat[i, r] = regroup(nc, feat_pool, rows, "grouped_batch%d" % i)
 
         def affinity(r):
             for i in range(ROUND_B):
@@ -243,22 +243,29 @@ def tile_sgcam_pa_t_kernel(
                 nc.sync.dma_start(out=out[ROUND_B * r + i].rearrange("(c p) m -> p c m", p=P), in_=result[:])
 
         with tc.manual_schedule():
-            spread(0)
-            regroup_x(0)
             permute_weights(0)
+            regroup_x(0)
             project(0, 0)
+            spread(0)
             permute_weights(1)
             project(0, 1)
-            regroup_x(1)
-            for r in range(1, SPREAD_LEAD):
+            for r in range(1, LEAD):
+                regroup_x(r)
                 spread(r)
+                project(r, 0)
+                project(r, 1)
+            regroup_x(LEAD)
+            spread(LEAD)
             for r in range(ROUNDS):
-                load_round(r + LOADS_AHEAD)
-                if r + 1 < ROUNDS:
-                    project(r + 1, 0)
-                    project(r + 1, 1)
-                spread(r + SPREAD_LEAD)
-                regroup_features(r)
-                regroup_x(r + GROUP_LEAD)
+                for side in range(SIDES):
+                    load(side, r + LOADS_AHEAD)
+                if r + LEAD < ROUNDS:
+                    project(r + LEAD, 0)
+                spread(r + GROUP_LEAD)
+                regroup_features(r, 0)
                 empty_direct(r + 1)
+                regroup_x(r + GROUP_LEAD)
+                regroup_features(r, 1)
+                if r + LEAD < ROUNDS:
+                    project(r + LEAD, 1)
                 affinity(r)

@@ -39,10 +39,8 @@ def regroup(nc, pool, rows, name):
     return grouped
 
 
-def regroup_one(nc, grouped, rows):
-    nc.vector.tensor_copy(
-        out=grouped.rearrange("p (c i) j -> p c j i", i=RUN), in_=rows.rearrange("p j (c i) -> p c j i", i=RUN)
-    )
+def regroup_one(copy, grouped, rows):
+    copy(out=grouped.rearrange("p (c i) j -> p c j i", i=RUN), in_=rows.rearrange("p j (c i) -> p c j i", i=RUN))
 
 
 def quantise(nc, pool, grouped, name):
@@ -80,6 +78,7 @@ def tile_sgcam_pa_t_kernel(
         grouped_in = {}
         planes = {}
         grouped_feat = {}
+        side_left = {}
         direct_banks = {}
 
         def load(side, r):
@@ -95,17 +94,25 @@ def tile_sgcam_pa_t_kernel(
         w_codes = consts.tile([P, SIDES, CHANNELS], U32, align_bytes=64, name="w_codes")
         w_planes = consts.tile([P, SIDES, CHANNELS], U8, align_bytes=64, name="w_planes")
         nc.vector.memset(w_planes_raw[:].rearrange("p s c -> p (s c)").bitcast(I32), 0)
-        for side in range(SIDES):
+        def load_scales(side):
             for quadrant in range(4):
                 nc.sync.dma_start(
                     out=w_planes_raw[32 * quadrant : 32 * quadrant + 4, side].bitcast(I32),
                     in_=weight_scales[side][0, 4 * quadrant : 4 * quadrant + 4, :].bitcast(I32),
                 )
+
+        def load_codes(side):
             nc.sync.dma_start(
                 out=w_codes_raw[:, side],
                 in_=weight_words[side][0].rearrange("p n t -> p (n t)").bitcast(I32),
             )
-            load(side, 0)
+
+        load_codes(0)
+        load(0, 0)
+        load_scales(0)
+        load(1, 0)
+        load_codes(1)
+        load_scales(1)
         for r in range(1, LOADS_AHEAD):
             for side in range(SIDES):
                 load(side, r)
@@ -118,11 +125,13 @@ def tile_sgcam_pa_t_kernel(
             nc.scalar.dma_start(out=cols[:], in_=biases[side].rearrange("(p t) -> p t", t=PACK))
             bias.append(cols)
 
-        def permute_weights(side):
+        def permute_codes(side):
             nc.vector.tensor_copy(
                 out=w_codes[:, side].bitcast(I32).rearrange("p (t m) -> p t m", t=PACK),
                 in_=w_codes_raw[:, side].rearrange("p (m t) -> p t m", t=PACK),
             )
+
+        def permute_scales(side):
             nc.vector.tensor_copy(
                 out=w_planes[:, side].rearrange("p (t m) -> p t m", t=PACK),
                 in_=w_planes_raw[:, side].rearrange("p (m t) -> p t m", t=PACK),
@@ -173,17 +182,23 @@ def tile_sgcam_pa_t_kernel(
         def is_direct(r):
             return r < ROUNDS and r % DIRECT_EVERY != 0
 
+        def project_batch(r, side, b, codes, scales):
+            for pair in range(PACK // 2):
+                acc = psum.tile([P, 2, POINTS], F32, name="bank")
+                for k in range(2):
+                    multiply(acc[:, k, :], side, 2 * pair + k, codes[:, b, :], scales[:, b, :])
+                for k in range(2):
+                    add_bias(planes[r][:, 2 * pair + k, side, b, :], acc[:, k, :], side, 2 * pair + k)
+
         def project(r, side):
             if side == 0:
                 planes[r] = planes_pool.tile([P, PACK, SIDES, ROUND_B, POINTS], BF16, name="planes")
             codes, scales = quantise(nc, work, grouped_in[side, r], side_names[side])
-            if side == 1 and is_direct(r):
-                for pair in range(PACK // 2):
-                    acc = psum.tile([P, 2, POINTS], F32, name="bank")
-                    for k in range(2):
-                        multiply(acc[:, k, :], side, 2 * pair + k, codes[:, 0, :], scales[:, 0, :])
-                    for k in range(2):
-                        add_bias(planes[r][:, 2 * pair + k, side, 0, :], acc[:, k, :], side, 2 * pair + k)
+            if side == 1 and r == ROUNDS - 1:
+                for b in range(ROUND_B):
+                    project_batch(r, side, b, codes, scales)
+            elif side == 1 and is_direct(r):
+                project_batch(r, side, 0, codes, scales)
                 direct_banks[r] = []
                 for c in range(ROW_TILES):
                     points = slice(P * c, P * (c + 1))
@@ -215,10 +230,18 @@ def tile_sgcam_pa_t_kernel(
                     op=ALU.add,
                 )
             grouped_feat[1, r] = grouped
+            side_left[1, r] = 0
+
+        def regroup_ahead(r):
+            grouped = feat_pool.tile([P, SIDES, POINTS, PACK], BF16, align_bytes=64, name="grouped_batch1")
+            regroup_one(nc.scalar.copy, grouped[:, 0], planes[r][:, :, 0, 1, :])
+            grouped_feat[1, r] = grouped
+            side_left[1, r] = 1
 
         def regroup_features(r, i):
             if (i, r) in grouped_feat:
-                regroup_one(nc, grouped_feat[i, r][:, 0], planes[r][:, :, 0, i, :])
+                side = side_left[i, r]
+                regroup_one(nc.vector.tensor_copy, grouped_feat[i, r][:, side], planes[r][:, :, side, i, :])
             else:
                 rows = planes[r][:, :, :, i, :].rearrange("p t s n -> p s t n")
                 grouped_feat[i, r] = regroup(nc, feat_pool, rows, "grouped_batch%d" % i)
@@ -226,8 +249,14 @@ def tile_sgcam_pa_t_kernel(
         def affinity(r):
             for i in range(ROUND_B):
                 codes, scales = quantise(nc, work, grouped_feat[i, r], "batch%d" % i)
-                prod = psum.tile([P, ROW_TILES, POINTS], F32, name="bank")
+                last = r == ROUNDS - 1 and i == ROUND_B - 1
+                result = result_pool.tile([P, ROW_TILES, POINTS], F32, name="result")
+                view = out[ROUND_B * r + i].rearrange("(c p) m -> p c m", p=P)
+                if not last:
+                    prod = psum.tile([P, ROW_TILES, POINTS], F32, name="bank")
                 for c in range(ROW_TILES):
+                    if last:
+                        prod = psum.tile([P, ROW_TILES, POINTS], F32, name="bank")
                     rows_c = slice(P * c, P * (c + 1))
                     nc.tensor.matmul_mx(
                         out=prod[:, c, :],
@@ -238,16 +267,28 @@ def tile_sgcam_pa_t_kernel(
                         start=True,
                         stop=True,
                     )
-                result = result_pool.tile([P, ROW_TILES, POINTS], F32, name="result")
-                nc.scalar.activation(out=result[:], in_=prod[:], func=ACT.Copy, scale=1.0 / POINTS)
-                nc.sync.dma_start(out=out[ROUND_B * r + i].rearrange("(c p) m -> p c m", p=P), in_=result[:])
+                    if last:
+                        if c == 0:
+                            nc.scalar.activation(
+                                out=result[:, c], in_=prod[:, c], func=ACT.Copy, scale=1.0 / POINTS
+                            )
+                        else:
+                            nc.vector.tensor_scalar(
+                                out=result[:, c], in0=prod[:, c], scalar1=1.0 / POINTS, scalar2=None, op0=ALU.mult
+                            )
+                        nc.sync.dma_start(out=view[:, c], in_=result[:, c])
+                if not last:
+                    nc.scalar.activation(out=result[:], in_=prod[:], func=ACT.Copy, scale=1.0 / POINTS)
+                    nc.sync.dma_start(out=view, in_=result[:])
 
         with tc.manual_schedule():
-            permute_weights(0)
+            permute_codes(0)
             regroup_x(0)
+            permute_scales(0)
             project(0, 0)
             spread(0)
-            permute_weights(1)
+            permute_codes(1)
+            permute_scales(1)
             project(0, 1)
             for r in range(1, LEAD):
                 regroup_x(r)
@@ -268,4 +309,6 @@ def tile_sgcam_pa_t_kernel(
                 regroup_features(r, 1)
                 if r + LEAD < ROUNDS:
                     project(r + LEAD, 1)
+                if r == ROUNDS - 2:
+                    regroup_ahead(ROUNDS - 1)
                 affinity(r)

@@ -26,7 +26,7 @@ RUN = 8
 LEAD = 2
 GROUP_LEAD = LEAD + 1
 LOADS_AHEAD = GROUP_LEAD + 2
-DIRECT_EVERY = 3
+DIRECT_EVERY = 2
 
 FLOPS = 2 * BATCHES * POINTS * CHANNELS * (2 * CHANNELS + POINTS)
 
@@ -76,6 +76,7 @@ def tile_sgcam_pa_t_kernel(
 
         raw = {}
         grouped_in = {}
+        mx_in = {}
         planes = {}
         grouped_feat = {}
         side_left = {}
@@ -107,24 +108,25 @@ def tile_sgcam_pa_t_kernel(
                 in_=weight_words[side][0].rearrange("p n t -> p (n t)").bitcast(I32),
             )
 
+        bias = [consts.tile([P, PACK], BF16, name="bias_" + name) for name in side_names]
+
+        def load_bias(side):
+            nc.sync.dma_start(out=bias[side][:], in_=biases[side].rearrange("(p t) -> p t", t=PACK))
+
         load_codes(0)
         load(0, 0)
         load_scales(0)
         load(1, 0)
+        load_bias(0)
         load_codes(1)
         load_scales(1)
+        load_bias(1)
         for r in range(1, LOADS_AHEAD):
             for side in range(SIDES):
                 load(side, r)
 
         identity = consts.tile([P, P], BF16, name="identity")
         make_identity(nc, identity[:])
-        bias = []
-        for side in range(SIDES):
-            cols = consts.tile([P, PACK], BF16, name="bias_" + side_names[side])
-            nc.scalar.dma_start(out=cols[:], in_=biases[side].rearrange("(p t) -> p t", t=PACK))
-            bias.append(cols)
-
         def permute_codes(side):
             nc.vector.tensor_copy(
                 out=w_codes[:, side].bitcast(I32).rearrange("p (t m) -> p t m", t=PACK),
@@ -158,6 +160,12 @@ def tile_sgcam_pa_t_kernel(
                 nc.scalar.copy(out=grouped[:, b], in_=bank[:])
             grouped_in[1, r] = grouped
 
+        def regroup_first_x2():
+            grouped = in_pool.tile([P, ROUND_B, POINTS, PACK], BF16, align_bytes=64, name="grouped_phi")
+            for b, copy in enumerate((nc.scalar.copy, nc.vector.tensor_copy)):
+                regroup_one(copy, grouped[:, b], raw[1, 0][:, b])
+            grouped_in[1, 0] = grouped
+
         def regroup_x(r):
             if r < ROUNDS:
                 grouped_in[0, r] = regroup(nc, in_pool, raw[0, r][:], "grouped_theta")
@@ -180,7 +188,7 @@ def tile_sgcam_pa_t_kernel(
             )
 
         def is_direct(r):
-            return r < ROUNDS and r % DIRECT_EVERY != 0
+            return r < ROUNDS - 1 and r % DIRECT_EVERY == 1
 
         def project_batch(r, side, b, codes, scales):
             for pair in range(PACK // 2):
@@ -190,10 +198,15 @@ def tile_sgcam_pa_t_kernel(
                 for k in range(2):
                     add_bias(planes[r][:, 2 * pair + k, side, b, :], acc[:, k, :], side, 2 * pair + k)
 
+        def quantise_input(r, side):
+            mx_in[side, r] = quantise(nc, work, grouped_in[side, r], side_names[side])
+
         def project(r, side):
             if side == 0:
                 planes[r] = planes_pool.tile([P, PACK, SIDES, ROUND_B, POINTS], BF16, name="planes")
-            codes, scales = quantise(nc, work, grouped_in[side, r], side_names[side])
+            if (side, r) not in mx_in:
+                quantise_input(r, side)
+            codes, scales = mx_in[side, r]
             if side == 1 and r == ROUNDS - 1:
                 for b in range(ROUND_B):
                     project_batch(r, side, b, codes, scales)
@@ -233,10 +246,13 @@ def tile_sgcam_pa_t_kernel(
             side_left[1, r] = 0
 
         def regroup_ahead(r):
-            grouped = feat_pool.tile([P, SIDES, POINTS, PACK], BF16, align_bytes=64, name="grouped_batch1")
-            regroup_one(nc.scalar.copy, grouped[:, 0], planes[r][:, :, 0, 1, :])
-            grouped_feat[1, r] = grouped
-            side_left[1, r] = 1
+            for i in range(ROUND_B):
+                grouped = feat_pool.tile(
+                    [P, SIDES, POINTS, PACK], BF16, align_bytes=64, name="grouped_batch%d" % i
+                )
+                regroup_one(nc.scalar.copy, grouped[:, 0], planes[r][:, :, 0, i, :])
+                grouped_feat[i, r] = grouped
+                side_left[i, r] = 1
 
         def regroup_features(r, i):
             if (i, r) in grouped_feat:
@@ -285,8 +301,9 @@ def tile_sgcam_pa_t_kernel(
             permute_codes(0)
             regroup_x(0)
             permute_scales(0)
+            quantise_input(0, 0)
+            regroup_first_x2()
             project(0, 0)
-            spread(0)
             permute_codes(1)
             permute_scales(1)
             project(0, 1)

@@ -26,32 +26,24 @@ RUN = 8
 LEAD = 2
 GROUP_LEAD = LEAD + 1
 LOADS_AHEAD = GROUP_LEAD + 2
-DIRECT_EVERY = 2
+DIRECT_EVERY = 4
 
 FLOPS = 2 * BATCHES * POINTS * CHANNELS * (2 * CHANNELS + POINTS)
 
 
-def regroup(nc, pool, rows, name):
-    grouped = pool.tile([P, 2, POINTS, PACK], BF16, align_bytes=64, name=name)
-    src = rows.rearrange("p g j (c i) -> p g c j i", i=RUN)
-    dst = grouped[:].rearrange("p g (c i) j -> p g c j i", i=RUN)
-    nc.vector.tensor_copy(out=dst, in_=src)
-    return grouped
+def regroup(nc, grouped, rows):
+    nc.vector.tensor_copy(
+        out=grouped.rearrange("p g (c i) j -> p g c j i", i=RUN),
+        in_=rows.rearrange("p g j (c i) -> p g c j i", i=RUN),
+    )
 
 
 def regroup_one(copy, grouped, rows):
     copy(out=grouped.rearrange("p (c i) j -> p c j i", i=RUN), in_=rows.rearrange("p j (c i) -> p c j i", i=RUN))
 
 
-def quantise(nc, pool, grouped, name):
-    codes = pool.tile([P, 2, POINTS], U32, align_bytes=64, name="codes_" + name)
-    scales = pool.tile([P, 2, POINTS], U8, align_bytes=64, name="scales_" + name)
-    nc.vector.quantize_mx(
-        out=codes[:].rearrange("p g n -> p (g n)").bitcast(FP8X4),
-        scales=scales[:].rearrange("p g n -> p (g n)"),
-        in_=grouped[:].rearrange("p g n j -> p (g n j)"),
-    )
-    return codes, scales
+def quantise(nc, codes, scales, grouped):
+    nc.vector.quantize_mx(out=codes.bitcast(FP8X4), scales=scales, in_=grouped)
 
 
 def tile_sgcam_pa_t_kernel(
@@ -139,11 +131,18 @@ def tile_sgcam_pa_t_kernel(
                 in_=w_planes_raw[:, side].rearrange("p (m t) -> p t m", t=PACK),
             )
 
+        def regroup_in(side, r):
+            grouped = in_pool.tile(
+                [P, ROUND_B, POINTS, PACK], BF16, align_bytes=64, name="grouped_" + side_names[side]
+            )
+            regroup(nc, grouped[:], raw[side, r][:])
+            grouped_in[side, r] = grouped
+
         def spread(r):
             if r >= ROUNDS:
                 return
             if r < LEAD:
-                grouped_in[1, r] = regroup(nc, in_pool, raw[1, r][:], "grouped_phi")
+                regroup_in(1, r)
                 return
             grouped = in_pool.tile([P, ROUND_B, POINTS, PACK], BF16, align_bytes=64, name="grouped_phi")
             for b in range(ROUND_B):
@@ -168,7 +167,7 @@ def tile_sgcam_pa_t_kernel(
 
         def regroup_x(r):
             if r < ROUNDS:
-                grouped_in[0, r] = regroup(nc, in_pool, raw[0, r][:], "grouped_theta")
+                regroup_in(0, r)
 
         def multiply(acc, side, t, codes, scales):
             chans = slice(P * t, P * (t + 1))
@@ -188,7 +187,7 @@ def tile_sgcam_pa_t_kernel(
             )
 
         def is_direct(r):
-            return r < ROUNDS - 1 and r % DIRECT_EVERY == 1
+            return r < ROUNDS - 1 and r % DIRECT_EVERY != 0
 
         def project_batch(r, side, b, codes, scales):
             for pair in range(PACK // 2):
@@ -199,7 +198,15 @@ def tile_sgcam_pa_t_kernel(
                     add_bias(planes[r][:, 2 * pair + k, side, b, :], acc[:, k, :], side, 2 * pair + k)
 
         def quantise_input(r, side):
-            mx_in[side, r] = quantise(nc, work, grouped_in[side, r], side_names[side])
+            codes = work.tile([P, ROUND_B, POINTS], U32, align_bytes=64, name="codes_" + side_names[side])
+            scales = work.tile([P, ROUND_B, POINTS], U8, align_bytes=64, name="scales_" + side_names[side])
+            quantise(
+                nc,
+                codes[:].rearrange("p b n -> p (b n)"),
+                scales[:].rearrange("p b n -> p (b n)"),
+                grouped_in[side, r][:].rearrange("p b n j -> p (b n j)"),
+            )
+            mx_in[side, r] = codes, scales
 
         def project(r, side):
             if side == 0:
@@ -231,40 +238,56 @@ def tile_sgcam_pa_t_kernel(
                     )
                     add_bias(planes[r][:, t, side].rearrange("p b n -> p (b n)"), acc[:], side, t)
 
+        def feat_tile(r):
+            if r not in grouped_feat:
+                grouped_feat[r] = feat_pool.tile(
+                    [P, ROUND_B, SIDES, POINTS, PACK], BF16, align_bytes=64, name="grouped_feat"
+                )
+            return grouped_feat[r]
+
         def empty_direct(r):
             if not is_direct(r):
                 return
-            grouped = feat_pool.tile([P, SIDES, POINTS, PACK], BF16, align_bytes=64, name="grouped_batch1")
             for c in range(ROW_TILES):
                 nc.vector.tensor_tensor(
-                    out=grouped[:, 1, P * c : P * (c + 1), :],
+                    out=feat_tile(r)[:, 1, 1, P * c : P * (c + 1), :],
                     in0=direct_banks[r][c][:].rearrange("p t n -> p n t"),
                     in1=bias[1][:].unsqueeze(1).to_broadcast([P, P, PACK]),
                     op=ALU.add,
                 )
-            grouped_feat[1, r] = grouped
             side_left[1, r] = 0
 
         def regroup_ahead(r):
-            for i in range(ROUND_B):
-                grouped = feat_pool.tile(
-                    [P, SIDES, POINTS, PACK], BF16, align_bytes=64, name="grouped_batch%d" % i
-                )
-                regroup_one(nc.scalar.copy, grouped[:, 0], planes[r][:, :, 0, i, :])
-                grouped_feat[i, r] = grouped
-                side_left[i, r] = 1
+            regroup_one(nc.scalar.copy, feat_tile(r)[:, 1, 0], planes[r][:, :, 0, 1, :])
+            side_left[1, r] = 1
 
         def regroup_features(r, i):
-            if (i, r) in grouped_feat:
+            if (i, r) in side_left:
                 side = side_left[i, r]
-                regroup_one(nc.vector.tensor_copy, grouped_feat[i, r][:, side], planes[r][:, :, side, i, :])
+                regroup_one(nc.vector.tensor_copy, feat_tile(r)[:, i, side], planes[r][:, :, side, i, :])
             else:
-                rows = planes[r][:, :, :, i, :].rearrange("p t s n -> p s t n")
-                grouped_feat[i, r] = regroup(nc, feat_pool, rows, "grouped_batch%d" % i)
+                regroup(nc, feat_tile(r)[:, i], planes[r][:, :, :, i, :].rearrange("p t s n -> p s t n"))
 
         def affinity(r):
+            all_codes = work.tile([P, ROUND_B, SIDES, POINTS], U32, align_bytes=64, name="codes_feat")
+            all_scales = work.tile([P, ROUND_B, SIDES, POINTS], U8, align_bytes=64, name="scales_feat")
+            grouped = feat_tile(r)
+            if r < ROUNDS - 1:
+                quantise(
+                    nc,
+                    all_codes[:].rearrange("p b s n -> p (b s n)"),
+                    all_scales[:].rearrange("p b s n -> p (b s n)"),
+                    grouped[:].rearrange("p b s n j -> p (b s n j)"),
+                )
             for i in range(ROUND_B):
-                codes, scales = quantise(nc, work, grouped_feat[i, r], "batch%d" % i)
+                codes, scales = all_codes[:, i], all_scales[:, i]
+                if r == ROUNDS - 1:
+                    quantise(
+                        nc,
+                        codes.rearrange("p s n -> p (s n)"),
+                        scales.rearrange("p s n -> p (s n)"),
+                        grouped[:, i].rearrange("p s n j -> p (s n j)"),
+                    )
                 last = r == ROUNDS - 1 and i == ROUND_B - 1
                 result = result_pool.tile([P, ROW_TILES, POINTS], F32, name="result")
                 view = out[ROUND_B * r + i].rearrange("(c p) m -> p c m", p=P)

@@ -14,6 +14,7 @@ ALU = mybir.AluOpType
 
 P = 128
 PACK = 4
+SPAN = 8
 BATCHES = 32
 CHANNELS = P * PACK
 POINTS = 256
@@ -100,19 +101,23 @@ def tile_sgcam_pa_t_kernel(
                 in_=weight_words[side][0].rearrange("p n t -> p (n t)").bitcast(I32),
             )
 
-        bias = [consts.tile([P, PACK], BF16, name="bias_" + name) for name in side_names]
+        bias_rows = consts.tile([P, P], BF16, name="bias_rows")
+        nc.vector.memset(bias_rows[:].bitcast(I32), 0)
 
         def load_bias(side):
-            nc.sync.dma_start(out=bias[side][:], in_=biases[side].rearrange("(p t) -> p t", t=PACK))
+            nc.sync.dma_start(
+                out=bias_rows[PACK * side : PACK * (side + 1), :].rearrange("t (q i) -> t q i", i=SPAN),
+                in_=biases[side].rearrange("(q t i) -> t q i", t=PACK, i=SPAN),
+            )
 
         load_codes(0)
         load(0, 0)
         load_scales(0)
-        load(1, 0)
         load_bias(0)
+        load_bias(1)
+        load(1, 0)
         load_codes(1)
         load_scales(1)
-        load_bias(1)
         for r in range(1, LOADS_AHEAD):
             for side in range(SIDES):
                 load(side, r)
@@ -121,14 +126,14 @@ def tile_sgcam_pa_t_kernel(
         make_identity(nc, identity[:])
         def permute_codes(side):
             nc.vector.tensor_copy(
-                out=w_codes[:, side].bitcast(I32).rearrange("p (t m) -> p t m", t=PACK),
-                in_=w_codes_raw[:, side].rearrange("p (m t) -> p t m", t=PACK),
+                out=w_codes[:, side].bitcast(I32).rearrange("p (t q i) -> p t q i", t=PACK, i=SPAN),
+                in_=w_codes_raw[:, side].rearrange("p (q t i) -> p t q i", t=PACK, i=SPAN),
             )
 
         def permute_scales(side):
             nc.vector.tensor_copy(
-                out=w_planes[:, side].rearrange("p (t m) -> p t m", t=PACK),
-                in_=w_planes_raw[:, side].rearrange("p (m t) -> p t m", t=PACK),
+                out=w_planes[:, side].bitcast(I32).rearrange("p (t q i) -> p t q i", t=PACK, i=SPAN // 4),
+                in_=w_planes_raw[:, side].bitcast(I32).rearrange("p (q t i) -> p t q i", t=PACK, i=SPAN // 4),
             )
 
         def regroup_in(side, r):
@@ -138,26 +143,24 @@ def tile_sgcam_pa_t_kernel(
             regroup(nc, grouped[:], raw[side, r][:])
             grouped_in[side, r] = grouped
 
-        def spread(r):
+        def spread(r, b):
             if r >= ROUNDS:
                 return
-            if r < LEAD:
-                regroup_in(1, r)
-                return
-            grouped = in_pool.tile([P, ROUND_B, POINTS, PACK], BF16, align_bytes=64, name="grouped_phi")
-            for b in range(ROUND_B):
-                bank = psum.tile([P, POINTS, PACK], BF16, name="bank")
-                for c in range(ROW_TILES):
-                    points = slice(P * c, P * (c + 1))
-                    nc.tensor.matmul(
-                        bank[:, points, :].rearrange("p n j -> p j n"),
-                        lhsT=identity[:],
-                        rhs=raw[1, r][:, b, :, points],
-                        start=True,
-                        stop=True,
-                    )
-                nc.scalar.copy(out=grouped[:, b], in_=bank[:])
-            grouped_in[1, r] = grouped
+            if b == 0:
+                grouped_in[1, r] = in_pool.tile(
+                    [P, ROUND_B, POINTS, PACK], BF16, align_bytes=64, name="grouped_phi"
+                )
+            bank = psum.tile([P, POINTS, PACK], BF16, name="bank")
+            for c in range(ROW_TILES):
+                points = slice(P * c, P * (c + 1))
+                nc.tensor.matmul(
+                    bank[:, points, :].rearrange("p n j -> p j n"),
+                    lhsT=identity[:],
+                    rhs=raw[1, r][:, b, :, points],
+                    start=True,
+                    stop=True,
+                )
+            nc.scalar.copy(out=grouped_in[1, r][:, b], in_=bank[:])
 
         def regroup_first_x2():
             grouped = in_pool.tile([P, ROUND_B, POINTS, PACK], BF16, align_bytes=64, name="grouped_phi")
@@ -183,7 +186,7 @@ def tile_sgcam_pa_t_kernel(
 
         def add_bias(plane, acc, side, t):
             nc.scalar.activation(
-                out=plane, in_=acc, func=ACT.Identity, bias=bias[side][:, t : t + 1], scale=1.0
+                out=plane, in_=acc, func=ACT.Identity, bias=bias[:, PACK * side + t : PACK * side + t + 1], scale=1.0
             )
 
         def is_direct(r):
@@ -252,7 +255,7 @@ def tile_sgcam_pa_t_kernel(
                 nc.vector.tensor_tensor(
                     out=feat_tile(r)[:, 1, 1, P * c : P * (c + 1), :],
                     in0=direct_banks[r][c][:].rearrange("p t n -> p n t"),
-                    in1=bias[1][:].unsqueeze(1).to_broadcast([P, P, PACK]),
+                    in1=bias[:, PACK : 2 * PACK].unsqueeze(1).to_broadcast([P, P, PACK]),
                     op=ALU.add,
                 )
             side_left[1, r] = 0
@@ -280,6 +283,8 @@ def tile_sgcam_pa_t_kernel(
                     grouped[:].rearrange("p b s n j -> p (b s n j)"),
                 )
             for i in range(ROUND_B):
+                if i == 1:
+                    spread(r + GROUP_LEAD, 1)
                 codes, scales = all_codes[:, i], all_scales[:, i]
                 if r == ROUNDS - 1:
                     quantise(
@@ -321,6 +326,10 @@ def tile_sgcam_pa_t_kernel(
                     nc.sync.dma_start(out=view, in_=result[:])
 
         with tc.manual_schedule():
+            bias_bank = psum.tile([P, P], BF16, name="bank")
+            nc.tensor.transpose(bias_bank[:], bias_rows[:], identity[:])
+            bias = consts.tile([P, SIDES * PACK], F32, name="bias")
+            nc.scalar.copy(out=bias[:], in_=bias_bank[:, 0 : SIDES * PACK])
             permute_codes(0)
             regroup_x(0)
             permute_scales(0)
@@ -332,17 +341,18 @@ def tile_sgcam_pa_t_kernel(
             project(0, 1)
             for r in range(1, LEAD):
                 regroup_x(r)
-                spread(r)
+                regroup_in(1, r)
                 project(r, 0)
                 project(r, 1)
             regroup_x(LEAD)
-            spread(LEAD)
+            for b in range(ROUND_B):
+                spread(LEAD, b)
             for r in range(ROUNDS):
                 for side in range(SIDES):
                     load(side, r + LOADS_AHEAD)
                 if r + LEAD < ROUNDS:
                     project(r + LEAD, 0)
-                spread(r + GROUP_LEAD)
+                spread(r + GROUP_LEAD, 0)
                 regroup_features(r, 0)
                 empty_direct(r + 1)
                 regroup_x(r + GROUP_LEAD)

@@ -27,7 +27,8 @@ RUN = 8
 LEAD = 2
 GROUP_LEAD = LEAD + 1
 LOADS_AHEAD = GROUP_LEAD + 2
-DIRECT_EVERY = 4
+DIRECT_CYCLE = 5
+DIRECT_ROUNDS = (1, 2, 4)
 
 FLOPS = 2 * BATCHES * POINTS * CHANNELS * (2 * CHANNELS + POINTS)
 
@@ -190,7 +191,7 @@ def tile_sgcam_pa_t_kernel(
             )
 
         def is_direct(r):
-            return r < ROUNDS - 1 and r % DIRECT_EVERY != 0
+            return r < ROUNDS - 1 and r % DIRECT_CYCLE in DIRECT_ROUNDS
 
         def project_batch(r, side, b, codes, scales):
             for pair in range(PACK // 2):

from contextlib import ExitStack

import concourse.mybir as mybir
from concourse.masks import make_identity

BF16 = mybir.dt.bfloat16
F32 = mybir.dt.float32
I32 = mybir.dt.int32
U32 = mybir.dt.uint32
U8 = mybir.dt.uint8
FP8X4 = mybir.dt.float8_e4m3fn_x4
ACT = mybir.ActivationFunctionType
ALU = mybir.AluOpType

P = 128
PACK = 4
SPAN = 8
BATCHES = 32
CHANNELS = P * PACK
POINTS = 256
SIDES = 2
ROUND_B = 2
ROUNDS = BATCHES // ROUND_B
COLS = ROUND_B * POINTS
ROW_TILES = POINTS // P
RUN = 8
LEAD = 2
GROUP_LEAD = LEAD + 1
LOADS_AHEAD = GROUP_LEAD + 2
DIRECT_CYCLE = 5
DIRECT_ROUNDS = (1, 2, 4)

FLOPS = 2 * BATCHES * POINTS * CHANNELS * (2 * CHANNELS + POINTS)


def regroup(nc, grouped, rows):
    nc.vector.tensor_copy(
        out=grouped.rearrange("p g (c i) j -> p g c j i", i=RUN),
        in_=rows.rearrange("p g j (c i) -> p g c j i", i=RUN),
    )


def regroup_one(copy, grouped, rows):
    copy(out=grouped.rearrange("p (c i) j -> p c j i", i=RUN), in_=rows.rearrange("p j (c i) -> p c j i", i=RUN))


def quantise(nc, codes, scales, grouped):
    nc.vector.quantize_mx(out=codes.bitcast(FP8X4), scales=scales, in_=grouped)


def tile_sgcam_pa_t_kernel(
    tc, x, x_2, theta_w_words, theta_w_scales, theta_b, phi_w_words, phi_w_scales, phi_b, out
):
    nc = tc.nc
    inputs = (x, x_2)
    weight_words = (theta_w_words, phi_w_words)
    weight_scales = (theta_w_scales, phi_w_scales)
    biases = (theta_b, phi_b)
    side_names = ("theta", "phi")

    with ExitStack() as ctx:
        consts = ctx.enter_context(tc.tile_pool(name="consts", bufs=1))
        raw_pool = ctx.enter_context(tc.tile_pool(name="raw", bufs=LOADS_AHEAD + 1))
        work = ctx.enter_context(tc.tile_pool(name="work", bufs=3))
        in_pool = ctx.enter_context(tc.tile_pool(name="in", bufs=3))
        feat_pool = ctx.enter_context(tc.tile_pool(name="feat", bufs=3))
        planes_pool = ctx.enter_context(tc.tile_pool(name="planes", bufs=LEAD + 2))
        result_pool = ctx.enter_context(tc.tile_pool(name="result", bufs=4))
        psum = ctx.enter_context(tc.psum_pool(name="psum", bufs=8))

        raw = {}
        grouped_in = {}
        mx_in = {}
        planes = {}
        grouped_feat = {}
        side_left = {}
        direct_banks = {}

        def load(side, r):
            if r < ROUNDS:
                raw[side, r] = raw_pool.tile([P, ROUND_B, PACK, POINTS], BF16, name="raw_" + side_names[side])
                nc.sync.dma_start(
                    out=raw[side, r][:].rearrange("p b j n -> p b (j n)"),
                    in_=inputs[side][ROUND_B * r : ROUND_B * (r + 1)].rearrange("b (p j) n -> p b (j n)", j=PACK),
                )

        w_codes_raw = consts.tile([P, SIDES, CHANNELS], I32, align_bytes=64, name="w_codes_raw")
        w_planes_raw = consts.tile([P, SIDES, CHANNELS], U8, align_bytes=64, name="w_planes_raw")
        w_codes = consts.tile([P, SIDES, CHANNELS], U32, align_bytes=64, name="w_codes")
        w_planes = consts.tile([P, SIDES, CHANNELS], U8, align_bytes=64, name="w_planes")
        nc.vector.memset(w_planes_raw[:].rearrange("p s c -> p (s c)").bitcast(I32), 0)
        def load_scales(side):
            for quadrant in range(4):
                nc.sync.dma_start(
                    out=w_planes_raw[32 * quadrant : 32 * quadrant + 4, side].bitcast(I32),
                    in_=weight_scales[side][0, 4 * quadrant : 4 * quadrant + 4, :].bitcast(I32),
                )

        def load_codes(side):
            nc.sync.dma_start(
                out=w_codes_raw[:, side],
                in_=weight_words[side][0].rearrange("p n t -> p (n t)").bitcast(I32),
            )

        bias_rows = consts.tile([P, P], BF16, name="bias_rows")
        nc.vector.memset(bias_rows[:].bitcast(I32), 0)

        def load_bias(side):
            nc.sync.dma_start(
                out=bias_rows[PACK * side : PACK * (side + 1), :].rearrange("t (q i) -> t q i", i=SPAN),
                in_=biases[side].rearrange("(q t i) -> t q i", t=PACK, i=SPAN),
            )

        load_codes(0)
        load(0, 0)
        load_scales(0)
        load_bias(0)
        load_bias(1)
        load(1, 0)
        load_codes(1)
        load_scales(1)
        for r in range(1, LOADS_AHEAD):
            for side in range(SIDES):
                load(side, r)

        identity = consts.tile([P, P], BF16, name="identity")
        make_identity(nc, identity[:])
        def permute_codes(side):
            nc.vector.tensor_copy(
                out=w_codes[:, side].bitcast(I32).rearrange("p (t q i) -> p t q i", t=PACK, i=SPAN),
                in_=w_codes_raw[:, side].rearrange("p (q t i) -> p t q i", t=PACK, i=SPAN),
            )

        def permute_scales(side):
            nc.vector.tensor_copy(
                out=w_planes[:, side].bitcast(I32).rearrange("p (t q i) -> p t q i", t=PACK, i=SPAN // 4),
                in_=w_planes_raw[:, side].bitcast(I32).rearrange("p (q t i) -> p t q i", t=PACK, i=SPAN // 4),
            )

        def regroup_in(side, r):
            grouped = in_pool.tile(
                [P, ROUND_B, POINTS, PACK], BF16, align_bytes=64, name="grouped_" + side_names[side]
            )
            regroup(nc, grouped[:], raw[side, r][:])
            grouped_in[side, r] = grouped

        def spread(r, b):
            if r >= ROUNDS:
                return
            if b == 0:
                grouped_in[1, r] = in_pool.tile(
                    [P, ROUND_B, POINTS, PACK], BF16, align_bytes=64, name="grouped_phi"
                )
            bank = psum.tile([P, POINTS, PACK], BF16, name="bank")
            for c in range(ROW_TILES):
                points = slice(P * c, P * (c + 1))
                nc.tensor.matmul(
                    bank[:, points, :].rearrange("p n j -> p j n"),
                    lhsT=identity[:],
                    rhs=raw[1, r][:, b, :, points],
                    start=True,
                    stop=True,
                )
            nc.scalar.copy(out=grouped_in[1, r][:, b], in_=bank[:])

        def regroup_first_x2():
            grouped = in_pool.tile([P, ROUND_B, POINTS, PACK], BF16, align_bytes=64, name="grouped_phi")
            for b, copy in enumerate((nc.scalar.copy, nc.vector.tensor_copy)):
                regroup_one(copy, grouped[:, b], raw[1, 0][:, b])
            grouped_in[1, 0] = grouped

        def regroup_x(r):
            if r < ROUNDS:
                regroup_in(0, r)

        def multiply(acc, side, t, codes, scales):
            chans = slice(P * t, P * (t + 1))
            nc.tensor.matmul_mx(
                out=acc,
                lhsT=w_codes[:, side, chans].bitcast(FP8X4),
                lhsT_scale=w_planes[:, side, chans],
                rhs=codes.bitcast(FP8X4),
                rhs_scale=scales,
                start=True,
                stop=True,
            )

        def add_bias(plane, acc, side, t):
            nc.scalar.activation(
                out=plane, in_=acc, func=ACT.Identity, bias=bias[:, PACK * side + t : PACK * side + t + 1], scale=1.0
            )

        def is_direct(r):
            return r < ROUNDS - 1 and r % DIRECT_CYCLE in DIRECT_ROUNDS

        def project_batch(r, side, b, codes, scales):
            for pair in range(PACK // 2):
                acc = psum.tile([P, 2, POINTS], F32, name="bank")
                for k in range(2):
                    multiply(acc[:, k, :], side, 2 * pair + k, codes[:, b, :], scales[:, b, :])
                for k in range(2):
                    add_bias(planes[r][:, 2 * pair + k, side, b, :], acc[:, k, :], side, 2 * pair + k)

        def quantise_input(r, side):
            codes = work.tile([P, ROUND_B, POINTS], U32, align_bytes=64, name="codes_" + side_names[side])
            scales = work.tile([P, ROUND_B, POINTS], U8, align_bytes=64, name="scales_" + side_names[side])
            quantise(
                nc,
                codes[:].rearrange("p b n -> p (b n)"),
                scales[:].rearrange("p b n -> p (b n)"),
                grouped_in[side, r][:].rearrange("p b n j -> p (b n j)"),
            )
            mx_in[side, r] = codes, scales

        def project(r, side):
            if side == 0:
                planes[r] = planes_pool.tile([P, PACK, SIDES, ROUND_B, POINTS], BF16, name="planes")
            if (side, r) not in mx_in:
                quantise_input(r, side)
            codes, scales = mx_in[side, r]
            if side == 1 and r == ROUNDS - 1:
                for b in range(ROUND_B):
                    project_batch(r, side, b, codes, scales)
            elif side == 1 and is_direct(r):
                project_batch(r, side, 0, codes, scales)
                direct_banks[r] = []
                for c in range(ROW_TILES):
                    points = slice(P * c, P * (c + 1))
                    acc = psum.tile([P, PACK, P], F32, name="bank")
                    for t in range(PACK):
                        multiply(acc[:, t, :], side, t, codes[:, 1, points], scales[:, 1, points])
                    direct_banks[r].append(acc)
            else:
                for t in range(PACK):
                    acc = psum.tile([P, COLS], F32, name="bank")
                    multiply(
                        acc[:],
                        side,
                        t,
                        codes[:].rearrange("p b n -> p (b n)"),
                        scales[:].rearrange("p b n -> p (b n)"),
                    )
                    add_bias(planes[r][:, t, side].rearrange("p b n -> p (b n)"), acc[:], side, t)

        def feat_tile(r):
            if r not in grouped_feat:
                grouped_feat[r] = feat_pool.tile(
                    [P, ROUND_B, SIDES, POINTS, PACK], BF16, align_bytes=64, name="grouped_feat"
                )
            return grouped_feat[r]

        def empty_direct(r):
            if not is_direct(r):
                return
            for c in range(ROW_TILES):
                nc.vector.tensor_tensor(
                    out=feat_tile(r)[:, 1, 1, P * c : P * (c + 1), :],
                    in0=direct_banks[r][c][:].rearrange("p t n -> p n t"),
                    in1=bias[:, PACK : 2 * PACK].unsqueeze(1).to_broadcast([P, P, PACK]),
                    op=ALU.add,
                )
            side_left[1, r] = 0

        def regroup_ahead(r):
            regroup_one(nc.scalar.copy, feat_tile(r)[:, 1, 0], planes[r][:, :, 0, 1, :])
            side_left[1, r] = 1

        def regroup_features(r, i):
            if (i, r) in side_left:
                side = side_left[i, r]
                regroup_one(nc.vector.tensor_copy, feat_tile(r)[:, i, side], planes[r][:, :, side, i, :])
            else:
                regroup(nc, feat_tile(r)[:, i], planes[r][:, :, :, i, :].rearrange("p t s n -> p s t n"))

        def affinity(r):
            all_codes = work.tile([P, ROUND_B, SIDES, POINTS], U32, align_bytes=64, name="codes_feat")
            all_scales = work.tile([P, ROUND_B, SIDES, POINTS], U8, align_bytes=64, name="scales_feat")
            grouped = feat_tile(r)
            if r < ROUNDS - 1:
                quantise(
                    nc,
                    all_codes[:].rearrange("p b s n -> p (b s n)"),
                    all_scales[:].rearrange("p b s n -> p (b s n)"),
                    grouped[:].rearrange("p b s n j -> p (b s n j)"),
                )
            for i in range(ROUND_B):
                if i == 1:
                    spread(r + GROUP_LEAD, 1)
                codes, scales = all_codes[:, i], all_scales[:, i]
                if r == ROUNDS - 1:
                    quantise(
                        nc,
                        codes.rearrange("p s n -> p (s n)"),
                        scales.rearrange("p s n -> p (s n)"),
                        grouped[:, i].rearrange("p s n j -> p (s n j)"),
                    )
                last = r == ROUNDS - 1 and i == ROUND_B - 1
                result = result_pool.tile([P, ROW_TILES, POINTS], F32, name="result")
                view = out[ROUND_B * r + i].rearrange("(c p) m -> p c m", p=P)
                if not last:
                    prod = psum.tile([P, ROW_TILES, POINTS], F32, name="bank")
                for c in range(ROW_TILES):
                    if last:
                        prod = psum.tile([P, ROW_TILES, POINTS], F32, name="bank")
                    rows_c = slice(P * c, P * (c + 1))
                    nc.tensor.matmul_mx(
                        out=prod[:, c, :],
                        lhsT=codes[:, 0, rows_c].bitcast(FP8X4),
                        lhsT_scale=scales[:, 0, rows_c],
                        rhs=codes[:, 1, :].bitcast(FP8X4),
                        rhs_scale=scales[:, 1, :],
                        start=True,
                        stop=True,
                    )
                    if last:
                        if c == 0:
                            nc.scalar.activation(
                                out=result[:, c], in_=prod[:, c], func=ACT.Copy, scale=1.0 / POINTS
                            )
                        else:
                            nc.vector.tensor_scalar(
                                out=result[:, c], in0=prod[:, c], scalar1=1.0 / POINTS, scalar2=None, op0=ALU.mult
                            )
                        nc.sync.dma_start(out=view[:, c], in_=result[:, c])
                if not last:
                    nc.scalar.activation(out=result[:], in_=prod[:], func=ACT.Copy, scale=1.0 / POINTS)
                    nc.sync.dma_start(out=view, in_=result[:])

        with tc.manual_schedule():
            bias_bank = psum.tile([P, P], BF16, name="bank")
            nc.tensor.transpose(bias_bank[:], bias_rows[:], identity[:])
            bias = consts.tile([P, SIDES * PACK], F32, name="bias")
            nc.scalar.copy(out=bias[:], in_=bias_bank[:, 0 : SIDES * PACK])
            permute_codes(0)
            regroup_x(0)
            permute_scales(0)
            quantise_input(0, 0)
            regroup_first_x2()
            project(0, 0)
            permute_codes(1)
            permute_scales(1)
            project(0, 1)
            for r in range(1, LEAD):
                regroup_x(r)
                regroup_in(1, r)
                project(r, 0)
                project(r, 1)
            regroup_x(LEAD)
            for b in range(ROUND_B):
                spread(LEAD, b)
            for r in range(ROUNDS):
                for side in range(SIDES):
                    load(side, r + LOADS_AHEAD)
                if r + LEAD < ROUNDS:
                    project(r + LEAD, 0)
                spread(r + GROUP_LEAD, 0)
                regroup_features(r, 0)
                empty_direct(r + 1)
                regroup_x(r + GROUP_LEAD)
                regroup_features(r, 1)
                if r + LEAD < ROUNDS:
                    project(r + LEAD, 1)
                if r == ROUNDS - 2:
                    regroup_ahead(ROUNDS - 1)
                affinity(r)
